import numpy as np
import ml_dtypes

BF16 = ml_dtypes.bfloat16


def bf(x):
    return np.asarray(x, np.float32).astype(BF16)


def f32(x):
    return np.asarray(x, np.float32)


def f64(x):
    return np.asarray(x).astype(np.float64)


def striped(idx):
    return np.tile(idx.reshape(-1, 16).T, (8, 1))


C, C2, S, N = 128, 256, 2048, 1024
DT = 0.1
GATE = 0.5


def setup_inputs():
    return {
        "base": f32(np.random.standard_normal((C, S))),
        "cur": bf(np.random.standard_normal((C, N))),
        "near": bf(np.random.standard_normal((C, N))),
        "far": bf(np.random.standard_normal((C, N))),
        "wl": bf(np.random.standard_normal((C2, C)) / np.sqrt(C2)),
        "bl": f32(0.1 * np.random.standard_normal((C, 1))),
        "wc": bf(np.random.standard_normal((C2, C)) / np.sqrt(C2)),
        "offs": striped(np.random.permutation(S)[:N]),
    }


def reference(base, cur, near, far, wl, bl, wc, offs):
    idx = offs[:16].T.reshape(-1)
    local = np.tanh(f64(wl)[:C].T @ f64(cur) + f64(wl)[C:].T @ f64(near) + f64(bl))
    distant = DT * np.tanh(f64(wc)[:C].T @ f64(cur) + f64(wc)[C:].T @ f64(far))
    out = f64(base).copy()
    out[:, idx] = f64(cur) + GATE * (local + distant)
    return out

@@ -1,0 +1,70 @@
+import concourse.mybir as mybir
+
+F32 = mybir.dt.float32
+BF16 = mybir.dt.bfloat16
+U16 = mybir.dt.uint16
+ADD = mybir.AluOpType.add
+MULT = mybir.AluOpType.mult
+TANH = mybir.ActivationFunctionType.Tanh
+
+C = 128
+S = 2048
+N = 1024
+CHUNK = 512
+GATE = 0.5
+DT = 0.1
+
+FLOPS = 2 * (2 * C) * C * N * 2
+
+
+def tile_moeconnectionprocessor_kernel(tc, base, cur, near, far, wl, bl, wc, offs, out):
+    nc = tc.nc
+    with (
+        tc.tile_pool(name="held", bufs=1) as held,
+        tc.psum_pool(name="psum", bufs=2) as psum,
+    ):
+        offsets = held.tile([C, N // 16], U16, name="offsets")
+        nc.sync.dma_start(offsets[:], offs)
+
+        wl_sb = held.tile([C, 2, C], BF16, name="wl_sb")
+        wc_sb = held.tile([C, 2, C], BF16, name="wc_sb")
+        cur_sb = held.tile([C, N], BF16, name="cur_sb")
+        near_sb = held.tile([C, N], BF16, name="near_sb")
+        far_sb = held.tile([C, N], BF16, name="far_sb")
+        bias = held.tile([C, 1], F32, name="bias")
+        window = held.tile([C, S], F32, name="window")
+
+        nc.sync.dma_start(wl_sb[:], wl.rearrange("(h k) c -> k h c", h=2))
+        nc.sync.dma_start(cur_sb[:], cur)
+        nc.sync.dma_start(near_sb[:], near)
+        nc.scalar.dma_start(bias[:], bl)
+        nc.scalar.dma_start(wc_sb[:], wc.rearrange("(h k) c -> k h c", h=2))
+        nc.scalar.dma_start(far_sb[:], far)
+        nc.gpsimd.dma_start(window[:], base)
+
+        cur_f32 = held.tile([C, N], F32, name="cur_f32")
+        nc.gpsimd.tensor_copy(cur_f32[:], cur_sb[:])
+
+        local = held.tile([C, N], F32, name="local")
+        distant = held.tile([C, N], F32, name="distant")
+        mix = held.tile([C, N], F32, name="mix")
+        for j in range(0, N, CHUNK):
+            cols = slice(j, j + CHUNK)
+
+            local_ps = psum.tile([C, CHUNK], F32, name="local_ps")
+            nc.tensor.matmul(local_ps[:], wl_sb[:, 0, :], cur_sb[:, cols], start=True, stop=False)
+            nc.tensor.matmul(local_ps[:], wl_sb[:, 1, :], near_sb[:, cols], start=False, stop=True)
+            distant_ps = psum.tile([C, CHUNK], F32, name="distant_ps")
+            nc.tensor.matmul(distant_ps[:], wc_sb[:, 0, :], cur_sb[:, cols], start=True, stop=False)
+            nc.tensor.matmul(distant_ps[:], wc_sb[:, 1, :], far_sb[:, cols], start=False, stop=True)
+
+            nc.scalar.activation(local[:, cols], local_ps[:], TANH, bias=bias[:])
+            nc.scalar.activation(distant[:, cols], distant_ps[:], TANH)
+
+            nc.vector.tensor_scalar(local[:, cols], local[:, cols], GATE, None, MULT)
+            nc.vector.scalar_tensor_tensor(
+                mix[:, cols], distant[:, cols], GATE * DT, local[:, cols], MULT, ADD
+            )
+
+        nc.vector.tensor_tensor(window[:].indirect(offsets[:]), cur_f32[:], mix[:], ADD)
+        nc.sync.dma_start(out, window[:])

@@ -23,27 +23,29 @@ def tile_moeconnectionprocessor_kernel(tc, base, cur, near, far, wl, bl, wc, off
         tc.tile_pool(name="held", bufs=1) as held,
         tc.psum_pool(name="psum", bufs=2) as psum,
     ):
-        offsets = held.tile([C, N // 16], U16, name="offsets")
-        nc.sync.dma_start(offsets[:], offs)
-
         wl_sb = held.tile([C, 2, C], BF16, name="wl_sb")
         wc_sb = held.tile([C, 2, C], BF16, name="wc_sb")
         cur_sb = held.tile([C, N], BF16, name="cur_sb")
         near_sb = held.tile([C, N], BF16, name="near_sb")
         far_sb = held.tile([C, N], BF16, name="far_sb")
         bias = held.tile([C, 1], F32, name="bias")
+        offsets = held.tile([C, N // 16], U16, name="offsets")
         window = held.tile([C, S], F32, name="window")
 
         nc.sync.dma_start(wl_sb[:], wl.rearrange("(h k) c -> k h c", h=2))
-        nc.sync.dma_start(cur_sb[:], cur)
-        nc.sync.dma_start(near_sb[:], near)
         nc.scalar.dma_start(bias[:], bl)
         nc.scalar.dma_start(wc_sb[:], wc.rearrange("(h k) c -> k h c", h=2))
-        nc.scalar.dma_start(far_sb[:], far)
-        nc.gpsimd.dma_start(window[:], base)
+        for j in range(0, N, CHUNK):
+            cols = slice(j, j + CHUNK)
+            nc.sync.dma_start(cur_sb[:, cols], cur[:, cols])
+            nc.sync.dma_start(near_sb[:, cols], near[:, cols])
+            nc.scalar.dma_start(far_sb[:, cols], far[:, cols])
+        nc.sync.dma_start(offsets[:], offs)
+        nc.sync.dma_start(window[:, : S // 2], base[:, : S // 2])
+        nc.scalar.dma_start(window[:, S // 2 :], base[:, S // 2 :])
 
         cur_f32 = held.tile([C, N], F32, name="cur_f32")
-        nc.gpsimd.tensor_copy(cur_f32[:], cur_sb[:])
+        nc.vector.tensor_copy(cur_f32[:], cur_sb[:])
 
         local = held.tile([C, N], F32, name="local")
         distant = held.tile([C, N], F32, name="distant")

@@ -10,9 +10,12 @@ TANH = mybir.ActivationFunctionType.Tanh
 C = 128
 S = 2048
 N = 1024
-CHUNK = 512
+CHUNK = 256
 GATE = 0.5
 DT = 0.1
+
+WARM_MATMULS = 4
+WARM_COLS = 512
 
 FLOPS = 2 * (2 * C) * C * N * 2
 
@@ -21,7 +24,8 @@ def tile_moeconnectionprocessor_kernel(tc, base, cur, near, far, wl, bl, wc, off
     nc = tc.nc
     with (
         tc.tile_pool(name="held", bufs=1) as held,
-        tc.psum_pool(name="psum", bufs=2) as psum,
+        tc.psum_pool(name="psum", bufs=3) as psum,
+        tc.psum_pool(name="warm_psum", bufs=1) as warm_psum,
     ):
         wl_sb = held.tile([C, 2, C], BF16, name="wl_sb")
         wc_sb = held.tile([C, 2, C], BF16, name="wc_sb")
@@ -33,16 +37,24 @@ def tile_moeconnectionprocessor_kernel(tc, base, cur, near, far, wl, bl, wc, off
         window = held.tile([C, S], F32, name="window")
 
         nc.sync.dma_start(wl_sb[:], wl.rearrange("(h k) c -> k h c", h=2))
+        nc.sync.dma_start(cur_sb[:], cur)
+        nc.sync.dma_start(near_sb[:], near)
         nc.scalar.dma_start(bias[:], bl)
         nc.scalar.dma_start(wc_sb[:], wc.rearrange("(h k) c -> k h c", h=2))
-        for j in range(0, N, CHUNK):
-            cols = slice(j, j + CHUNK)
-            nc.sync.dma_start(cur_sb[:, cols], cur[:, cols])
-            nc.sync.dma_start(near_sb[:, cols], near[:, cols])
-            nc.scalar.dma_start(far_sb[:, cols], far[:, cols])
+        nc.scalar.dma_start(far_sb[:], far)
         nc.sync.dma_start(offsets[:], offs)
-        nc.sync.dma_start(window[:, : S // 2], base[:, : S // 2])
-        nc.scalar.dma_start(window[:, S // 2 :], base[:, S // 2 :])
+        nc.sync.dma_start(window[:], base)
+
+        tanh_in = held.tile([C, 1], F32, name="tanh_in")
+        tanh_out = held.tile([C, 1], F32, name="tanh_out")
+        nc.gpsimd.memset(tanh_in[:], 0.0)
+        nc.scalar.activation(tanh_out[:], tanh_in[:], TANH)
+
+        zeros = held.tile([C, WARM_COLS], BF16, name="zeros")
+        nc.gpsimd.memset(zeros[:].bitcast(F32), 0.0)
+        warm_ps = warm_psum.tile([C, WARM_COLS], F32, name="warm_ps")
+        for i in range(WARM_MATMULS):
+            nc.tensor.matmul(warm_ps[:], zeros[:, :C], zeros[:], start=True, stop=True)
 
         cur_f32 = held.tile([C, N], F32, name="cur_f32")
         nc.vector.tensor_copy(cur_f32[:], cur_sb[:])

@@ -25,23 +25,23 @@ def tile_moeconnectionprocessor_kernel(tc, base, cur, near, far, wl, bl, wc, off
     with (
         tc.tile_pool(name="held", bufs=1) as held,
         tc.psum_pool(name="psum", bufs=3) as psum,
-        tc.psum_pool(name="warm_psum", bufs=1) as warm_psum,
+        tc.psum_pool(name="once_psum", bufs=1) as once_psum,
     ):
         wl_sb = held.tile([C, 2, C], BF16, name="wl_sb")
         wc_sb = held.tile([C, 2, C], BF16, name="wc_sb")
         cur_sb = held.tile([C, N], BF16, name="cur_sb")
         near_sb = held.tile([C, N], BF16, name="near_sb")
         far_sb = held.tile([C, N], BF16, name="far_sb")
-        bias = held.tile([C, 1], F32, name="bias")
+        bl_row = held.tile([1, C], F32, name="bl_row")
         offsets = held.tile([C, N // 16], U16, name="offsets")
         window = held.tile([C, S], F32, name="window")
 
-        nc.sync.dma_start(wl_sb[:], wl.rearrange("(h k) c -> k h c", h=2))
-        nc.sync.dma_start(cur_sb[:], cur)
-        nc.sync.dma_start(near_sb[:], near)
-        nc.scalar.dma_start(bias[:], bl)
+        nc.scalar.dma_start(bl_row[:], bl.rearrange("c one -> one c"))
         nc.scalar.dma_start(wc_sb[:], wc.rearrange("(h k) c -> k h c", h=2))
         nc.scalar.dma_start(far_sb[:], far)
+        nc.sync.dma_start(cur_sb[:], cur)
+        nc.sync.dma_start(wl_sb[:], wl.rearrange("(h k) c -> k h c", h=2))
+        nc.sync.dma_start(near_sb[:], near)
         nc.sync.dma_start(offsets[:], offs)
         nc.sync.dma_start(window[:], base)
 
@@ -52,32 +52,39 @@ def tile_moeconnectionprocessor_kernel(tc, base, cur, near, far, wl, bl, wc, off
 
         zeros = held.tile([C, WARM_COLS], BF16, name="zeros")
         nc.gpsimd.memset(zeros[:].bitcast(F32), 0.0)
-        warm_ps = warm_psum.tile([C, WARM_COLS], F32, name="warm_ps")
+        warm_ps = once_psum.tile([C, WARM_COLS], F32, name="warm_ps")
         for i in range(WARM_MATMULS):
             nc.tensor.matmul(warm_ps[:], zeros[:, :C], zeros[:], start=True, stop=True)
+
+        one = held.tile([1, 1], F32, name="one")
+        nc.gpsimd.memset(one[:], 1.0)
+        bias_ps = once_psum.tile([C, 1], F32, name="bias_ps")
+        nc.tensor.matmul(bias_ps[:], bl_row[:], one[:], start=True, stop=True)
+        bias = held.tile([C, 1], F32, name="bias")
+        nc.vector.tensor_copy(bias[:], bias_ps[:])
 
         cur_f32 = held.tile([C, N], F32, name="cur_f32")
         nc.vector.tensor_copy(cur_f32[:], cur_sb[:])
 
-        local = held.tile([C, N], F32, name="local")
         distant = held.tile([C, N], F32, name="distant")
+        local = held.tile([C, N], F32, name="local")
         mix = held.tile([C, N], F32, name="mix")
         for j in range(0, N, CHUNK):
             cols = slice(j, j + CHUNK)
 
-            local_ps = psum.tile([C, CHUNK], F32, name="local_ps")
-            nc.tensor.matmul(local_ps[:], wl_sb[:, 0, :], cur_sb[:, cols], start=True, stop=False)
-            nc.tensor.matmul(local_ps[:], wl_sb[:, 1, :], near_sb[:, cols], start=False, stop=True)
             distant_ps = psum.tile([C, CHUNK], F32, name="distant_ps")
             nc.tensor.matmul(distant_ps[:], wc_sb[:, 0, :], cur_sb[:, cols], start=True, stop=False)
             nc.tensor.matmul(distant_ps[:], wc_sb[:, 1, :], far_sb[:, cols], start=False, stop=True)
+            local_ps = psum.tile([C, CHUNK], F32, name="local_ps")
+            nc.tensor.matmul(local_ps[:], wl_sb[:, 0, :], cur_sb[:, cols], start=True, stop=False)
+            nc.tensor.matmul(local_ps[:], wl_sb[:, 1, :], near_sb[:, cols], start=False, stop=True)
 
-            nc.scalar.activation(local[:, cols], local_ps[:], TANH, bias=bias[:])
             nc.scalar.activation(distant[:, cols], distant_ps[:], TANH)
+            nc.scalar.activation(local[:, cols], local_ps[:], TANH, bias=bias[:])
 
-            nc.vector.tensor_scalar(local[:, cols], local[:, cols], GATE, None, MULT)
+            nc.vector.tensor_scalar(distant[:, cols], distant[:, cols], GATE * DT, None, MULT)
             nc.vector.scalar_tensor_tensor(
-                mix[:, cols], distant[:, cols], GATE * DT, local[:, cols], MULT, ADD
+                mix[:, cols], local[:, cols], GATE, distant[:, cols], MULT, ADD
             )
 
         nc.vector.tensor_tensor(window[:].indirect(offsets[:]), cur_f32[:], mix[:], ADD)

@@ -14,8 +14,10 @@ CHUNK = 256
 GATE = 0.5
 DT = 0.1
 
-WARM_MATMULS = 4
+WARM_MATMULS = 3
 WARM_COLS = 512
+
+HALF = N // 2
 
 FLOPS = 2 * (2 * C) * C * N * 2
 
@@ -25,23 +27,25 @@ def tile_moeconnectionprocessor_kernel(tc, base, cur, near, far, wl, bl, wc, off
     with (
         tc.tile_pool(name="held", bufs=1) as held,
         tc.psum_pool(name="psum", bufs=3) as psum,
-        tc.psum_pool(name="once_psum", bufs=1) as once_psum,
+        tc.psum_pool(name="warm_psum", bufs=1) as warm_psum,
     ):
         wl_sb = held.tile([C, 2, C], BF16, name="wl_sb")
         wc_sb = held.tile([C, 2, C], BF16, name="wc_sb")
         cur_sb = held.tile([C, N], BF16, name="cur_sb")
         near_sb = held.tile([C, N], BF16, name="near_sb")
         far_sb = held.tile([C, N], BF16, name="far_sb")
-        bl_row = held.tile([1, C], F32, name="bl_row")
+        bias = held.tile([C, 1], F32, name="bias")
         offsets = held.tile([C, N // 16], U16, name="offsets")
         window = held.tile([C, S], F32, name="window")
 
-        nc.scalar.dma_start(bl_row[:], bl.rearrange("c one -> one c"))
-        nc.scalar.dma_start(wc_sb[:], wc.rearrange("(h k) c -> k h c", h=2))
-        nc.scalar.dma_start(far_sb[:], far)
-        nc.sync.dma_start(cur_sb[:], cur)
         nc.sync.dma_start(wl_sb[:], wl.rearrange("(h k) c -> k h c", h=2))
-        nc.sync.dma_start(near_sb[:], near)
+        nc.scalar.dma_start(bias[:], bl)
+        nc.sync.dma_start(cur_sb[:, :HALF], cur[:, :HALF])
+        nc.scalar.dma_start(wc_sb[:], wc.rearrange("(h k) c -> k h c", h=2))
+        nc.sync.dma_start(near_sb[:, :HALF], near[:, :HALF])
+        nc.scalar.dma_start(far_sb[:], far)
+        nc.sync.dma_start(cur_sb[:, HALF:], cur[:, HALF:])
+        nc.sync.dma_start(near_sb[:, HALF:], near[:, HALF:])
         nc.sync.dma_start(offsets[:], offs)
         nc.sync.dma_start(window[:], base)
 
@@ -52,39 +56,32 @@ def tile_moeconnectionprocessor_kernel(tc, base, cur, near, far, wl, bl, wc, off
 
         zeros = held.tile([C, WARM_COLS], BF16, name="zeros")
         nc.gpsimd.memset(zeros[:].bitcast(F32), 0.0)
-        warm_ps = once_psum.tile([C, WARM_COLS], F32, name="warm_ps")
+        warm_ps = warm_psum.tile([C, WARM_COLS], F32, name="warm_ps")
         for i in range(WARM_MATMULS):
             nc.tensor.matmul(warm_ps[:], zeros[:, :C], zeros[:], start=True, stop=True)
-
-        one = held.tile([1, 1], F32, name="one")
-        nc.gpsimd.memset(one[:], 1.0)
-        bias_ps = once_psum.tile([C, 1], F32, name="bias_ps")
-        nc.tensor.matmul(bias_ps[:], bl_row[:], one[:], start=True, stop=True)
-        bias = held.tile([C, 1], F32, name="bias")
-        nc.vector.tensor_copy(bias[:], bias_ps[:])
 
         cur_f32 = held.tile([C, N], F32, name="cur_f32")
         nc.vector.tensor_copy(cur_f32[:], cur_sb[:])
 
-        distant = held.tile([C, N], F32, name="distant")
         local = held.tile([C, N], F32, name="local")
+        distant = held.tile([C, N], F32, name="distant")
         mix = held.tile([C, N], F32, name="mix")
         for j in range(0, N, CHUNK):
             cols = slice(j, j + CHUNK)
 
-            distant_ps = psum.tile([C, CHUNK], F32, name="distant_ps")
-            nc.tensor.matmul(distant_ps[:], wc_sb[:, 0, :], cur_sb[:, cols], start=True, stop=False)
-            nc.tensor.matmul(distant_ps[:], wc_sb[:, 1, :], far_sb[:, cols], start=False, stop=True)
             local_ps = psum.tile([C, CHUNK], F32, name="local_ps")
             nc.tensor.matmul(local_ps[:], wl_sb[:, 0, :], cur_sb[:, cols], start=True, stop=False)
             nc.tensor.matmul(local_ps[:], wl_sb[:, 1, :], near_sb[:, cols], start=False, stop=True)
+            distant_ps = psum.tile([C, CHUNK], F32, name="distant_ps")
+            nc.tensor.matmul(distant_ps[:], wc_sb[:, 0, :], cur_sb[:, cols], start=True, stop=False)
+            nc.tensor.matmul(distant_ps[:], wc_sb[:, 1, :], far_sb[:, cols], start=False, stop=True)
 
-            nc.scalar.activation(distant[:, cols], distant_ps[:], TANH)
             nc.scalar.activation(local[:, cols], local_ps[:], TANH, bias=bias[:])
+            nc.scalar.activation(distant[:, cols], distant_ps[:], TANH)
 
-            nc.vector.tensor_scalar(distant[:, cols], distant[:, cols], GATE * DT, None, MULT)
+            nc.vector.tensor_scalar(local[:, cols], local[:, cols], GATE, None, MULT)
             nc.vector.scalar_tensor_tensor(
-                mix[:, cols], local[:, cols], GATE, distant[:, cols], MULT, ADD
+                mix[:, cols], distant[:, cols], GATE * DT, local[:, cols], MULT, ADD
             )
 
         nc.vector.tensor_tensor(window[:].indirect(offsets[:]), cur_f32[:], mix[:], ADD)

@@ -10,14 +10,13 @@ TANH = mybir.ActivationFunctionType.Tanh
 C = 128
 S = 2048
 N = 1024
+HALF = N // 2
 CHUNK = 256
 GATE = 0.5
 DT = 0.1
 
 WARM_MATMULS = 3
 WARM_COLS = 512
-
-HALF = N // 2
 
 FLOPS = 2 * (2 * C) * C * N * 2
 
@@ -41,11 +40,14 @@ def tile_moeconnectionprocessor_kernel(tc, base, cur, near, far, wl, bl, wc, off
         nc.sync.dma_start(wl_sb[:], wl.rearrange("(h k) c -> k h c", h=2))
         nc.scalar.dma_start(bias[:], bl)
         nc.sync.dma_start(cur_sb[:, :HALF], cur[:, :HALF])
-        nc.scalar.dma_start(wc_sb[:], wc.rearrange("(h k) c -> k h c", h=2))
-        nc.sync.dma_start(near_sb[:, :HALF], near[:, :HALF])
+        nc.scalar.dma_start(near_sb[:, :HALF], near[:, :HALF])
+
+        nc.sync.dma_start(wc_sb[:], wc.rearrange("(h k) c -> k h c", h=2))
         nc.scalar.dma_start(far_sb[:], far)
+
         nc.sync.dma_start(cur_sb[:, HALF:], cur[:, HALF:])
-        nc.sync.dma_start(near_sb[:, HALF:], near[:, HALF:])
+        nc.scalar.dma_start(near_sb[:, HALF:], near[:, HALF:])
+
         nc.sync.dma_start(offsets[:], offs)
         nc.sync.dma_start(window[:], base)
 
@@ -61,28 +63,30 @@ def tile_moeconnectionprocessor_kernel(tc, base, cur, near, far, wl, bl, wc, off
             nc.tensor.matmul(warm_ps[:], zeros[:, :C], zeros[:], start=True, stop=True)
 
         cur_f32 = held.tile([C, N], F32, name="cur_f32")
-        nc.vector.tensor_copy(cur_f32[:], cur_sb[:])
-
         local = held.tile([C, N], F32, name="local")
         distant = held.tile([C, N], F32, name="distant")
         mix = held.tile([C, N], F32, name="mix")
-        for j in range(0, N, CHUNK):
-            cols = slice(j, j + CHUNK)
+        for first in range(0, N, HALF):
+            half = slice(first, first + HALF)
+            chunks = [slice(j, j + CHUNK) for j in range(first, first + HALF, CHUNK)]
 
-            local_ps = psum.tile([C, CHUNK], F32, name="local_ps")
-            nc.tensor.matmul(local_ps[:], wl_sb[:, 0, :], cur_sb[:, cols], start=True, stop=False)
-            nc.tensor.matmul(local_ps[:], wl_sb[:, 1, :], near_sb[:, cols], start=False, stop=True)
-            distant_ps = psum.tile([C, CHUNK], F32, name="distant_ps")
-            nc.tensor.matmul(distant_ps[:], wc_sb[:, 0, :], cur_sb[:, cols], start=True, stop=False)
-            nc.tensor.matmul(distant_ps[:], wc_sb[:, 1, :], far_sb[:, cols], start=False, stop=True)
+            nc.vector.tensor_copy(cur_f32[:, half], cur_sb[:, half])
 
-            nc.scalar.activation(local[:, cols], local_ps[:], TANH, bias=bias[:])
-            nc.scalar.activation(distant[:, cols], distant_ps[:], TANH)
+            for cols in chunks:
+                local_ps = psum.tile([C, CHUNK], F32, name="local_ps")
+                nc.tensor.matmul(local_ps[:], wl_sb[:, 0, :], cur_sb[:, cols], start=True, stop=False)
+                nc.tensor.matmul(local_ps[:], wl_sb[:, 1, :], near_sb[:, cols], start=False, stop=True)
+                nc.scalar.activation(local[:, cols], local_ps[:], TANH, bias=bias[:])
+                nc.vector.tensor_scalar(local[:, cols], local[:, cols], GATE, None, MULT)
 
-            nc.vector.tensor_scalar(local[:, cols], local[:, cols], GATE, None, MULT)
-            nc.vector.scalar_tensor_tensor(
-                mix[:, cols], distant[:, cols], GATE * DT, local[:, cols], MULT, ADD
-            )
+            for cols in chunks:
+                distant_ps = psum.tile([C, CHUNK], F32, name="distant_ps")
+                nc.tensor.matmul(distant_ps[:], wc_sb[:, 0, :], cur_sb[:, cols], start=True, stop=False)
+                nc.tensor.matmul(distant_ps[:], wc_sb[:, 1, :], far_sb[:, cols], start=False, stop=True)
+                nc.scalar.activation(distant[:, cols], distant_ps[:], TANH)
+                nc.vector.scalar_tensor_tensor(
+                    mix[:, cols], distant[:, cols], GATE * DT, local[:, cols], MULT, ADD
+                )
 
         nc.vector.tensor_tensor(window[:].indirect(offsets[:]), cur_f32[:], mix[:], ADD)
         nc.sync.dma_start(out, window[:])

@@ -88,5 +88,6 @@ def tile_moeconnectionprocessor_kernel(tc, base, cur, near, far, wl, bl, wc, off
                     mix[:, cols], distant[:, cols], GATE * DT, local[:, cols], MULT, ADD
                 )
 
+        nc.sync.dma_start(out[:, :N], mix[:])
         nc.vector.tensor_tensor(window[:].indirect(offsets[:]), cur_f32[:], mix[:], ADD)
         nc.sync.dma_start(out, window[:])

@@ -18,6 +18,8 @@ DT = 0.1
 WARM_MATMULS = 3
 WARM_COLS = 512
 
+TOUCH = 8
+
 FLOPS = 2 * (2 * C) * C * N * 2
 
 
@@ -88,6 +90,6 @@ def tile_moeconnectionprocessor_kernel(tc, base, cur, near, far, wl, bl, wc, off
                     mix[:, cols], distant[:, cols], GATE * DT, local[:, cols], MULT, ADD
                 )
 
-        nc.sync.dma_start(out[:, :N], mix[:])
+        nc.sync.dma_start(out[:, :TOUCH], mix[:, N - TOUCH :])
         nc.vector.tensor_tensor(window[:].indirect(offsets[:]), cur_f32[:], mix[:], ADD)
         nc.sync.dma_start(out, window[:])

@@ -64,32 +64,29 @@ def tile_moeconnectionprocessor_kernel(tc, base, cur, near, far, wl, bl, wc, off
         for i in range(WARM_MATMULS):
             nc.tensor.matmul(warm_ps[:], zeros[:, :C], zeros[:], start=True, stop=True)
 
-        cur_f32 = held.tile([C, N], F32, name="cur_f32")
         local = held.tile([C, N], F32, name="local")
         distant = held.tile([C, N], F32, name="distant")
-        mix = held.tile([C, N], F32, name="mix")
+        near_sum = held.tile([C, N], F32, name="near_sum")
+        far_step = held.tile([C, N], F32, name="far_step")
         for first in range(0, N, HALF):
-            half = slice(first, first + HALF)
             chunks = [slice(j, j + CHUNK) for j in range(first, first + HALF, CHUNK)]
-
-            nc.vector.tensor_copy(cur_f32[:, half], cur_sb[:, half])
 
             for cols in chunks:
                 local_ps = psum.tile([C, CHUNK], F32, name="local_ps")
                 nc.tensor.matmul(local_ps[:], wl_sb[:, 0, :], cur_sb[:, cols], start=True, stop=False)
                 nc.tensor.matmul(local_ps[:], wl_sb[:, 1, :], near_sb[:, cols], start=False, stop=True)
                 nc.scalar.activation(local[:, cols], local_ps[:], TANH, bias=bias[:])
-                nc.vector.tensor_scalar(local[:, cols], local[:, cols], GATE, None, MULT)
+                nc.vector.scalar_tensor_tensor(
+                    near_sum[:, cols], local[:, cols], GATE, cur_sb[:, cols], MULT, ADD
+                )
 
             for cols in chunks:
                 distant_ps = psum.tile([C, CHUNK], F32, name="distant_ps")
                 nc.tensor.matmul(distant_ps[:], wc_sb[:, 0, :], cur_sb[:, cols], start=True, stop=False)
                 nc.tensor.matmul(distant_ps[:], wc_sb[:, 1, :], far_sb[:, cols], start=False, stop=True)
                 nc.scalar.activation(distant[:, cols], distant_ps[:], TANH)
-                nc.vector.scalar_tensor_tensor(
-                    mix[:, cols], distant[:, cols], GATE * DT, local[:, cols], MULT, ADD
-                )
+                nc.vector.tensor_scalar(far_step[:, cols], distant[:, cols], GATE * DT, None, MULT)
 
-        nc.sync.dma_start(out[:, :TOUCH], mix[:, N - TOUCH :])
-        nc.vector.tensor_tensor(window[:].indirect(offsets[:]), cur_f32[:], mix[:], ADD)
+        nc.sync.dma_start(out[:, :TOUCH], far_step[:, N - TOUCH :])
+        nc.vector.tensor_tensor(window[:].indirect(offsets[:]), near_sum[:], far_step[:], ADD)
         nc.sync.dma_start(out, window[:])

@@ -18,6 +18,8 @@ DT = 0.1
 WARM_MATMULS = 3
 WARM_COLS = 512
 
+BLOCK = 32
+
 TOUCH = 8
 
 FLOPS = 2 * (2 * C) * C * N * 2
@@ -35,12 +37,16 @@ def tile_moeconnectionprocessor_kernel(tc, base, cur, near, far, wl, bl, wc, off
         cur_sb = held.tile([C, N], BF16, name="cur_sb")
         near_sb = held.tile([C, N], BF16, name="near_sb")
         far_sb = held.tile([C, N], BF16, name="far_sb")
-        bias = held.tile([C, 1], F32, name="bias")
+        bias_rows = held.tile([C, BLOCK], F32, name="bias_rows", align_bytes=64)
+        bias_cols = held.tile([C, BLOCK], F32, name="bias_cols", align_bytes=64)
+        bias = bias_cols[:, 0:1]
         offsets = held.tile([C, N // 16], U16, name="offsets")
         window = held.tile([C, S], F32, name="window")
 
+        nc.gpsimd.memset(bias_rows[:], 0.0)
+
         nc.sync.dma_start(wl_sb[:], wl.rearrange("(h k) c -> k h c", h=2))
-        nc.scalar.dma_start(bias[:], bl)
+        nc.scalar.dma_start(bias_rows[::BLOCK, :], bl.rearrange("(q i) o -> q (i o)", i=BLOCK))
         nc.sync.dma_start(cur_sb[:, :HALF], cur[:, :HALF])
         nc.scalar.dma_start(near_sb[:, :HALF], near[:, :HALF])
 
@@ -64,6 +70,8 @@ def tile_moeconnectionprocessor_kernel(tc, base, cur, near, far, wl, bl, wc, off
         for i in range(WARM_MATMULS):
             nc.tensor.matmul(warm_ps[:], zeros[:, :C], zeros[:], start=True, stop=True)
 
+        nc.vector.transpose(bias_cols[:], bias_rows[:])
+
         local = held.tile([C, N], F32, name="local")
         distant = held.tile([C, N], F32, name="distant")
         near_sum = held.tile([C, N], F32, name="near_sum")
@@ -75,7 +83,7 @@ def tile_moeconnectionprocessor_kernel(tc, base, cur, near, far, wl, bl, wc, off
                 local_ps = psum.tile([C, CHUNK], F32, name="local_ps")
                 nc.tensor.matmul(local_ps[:], wl_sb[:, 0, :], cur_sb[:, cols], start=True, stop=False)
                 nc.tensor.matmul(local_ps[:], wl_sb[:, 1, :], near_sb[:, cols], start=False, stop=True)
-                nc.scalar.activation(local[:, cols], local_ps[:], TANH, bias=bias[:])
+                nc.scalar.activation(local[:, cols], local_ps[:], TANH, bias=bias)
                 nc.vector.scalar_tensor_tensor(
                     near_sum[:, cols], local[:, cols], GATE, cur_sb[:, cols], MULT, ADD
                 )

import concourse.mybir as mybir

F32 = mybir.dt.float32
BF16 = mybir.dt.bfloat16
U16 = mybir.dt.uint16
ADD = mybir.AluOpType.add
MULT = mybir.AluOpType.mult
TANH = mybir.ActivationFunctionType.Tanh

C = 128
S = 2048
N = 1024
HALF = N // 2
CHUNK = 256
GATE = 0.5
DT = 0.1

WARM_MATMULS = 3
WARM_COLS = 512

BLOCK = 32

TOUCH = 8

FLOPS = 2 * (2 * C) * C * N * 2


def tile_moeconnectionprocessor_kernel(tc, base, cur, near, far, wl, bl, wc, offs, out):
    nc = tc.nc
    with (
        tc.tile_pool(name="held", bufs=1) as held,
        tc.psum_pool(name="psum", bufs=3) as psum,
        tc.psum_pool(name="warm_psum", bufs=1) as warm_psum,
    ):
        wl_sb = held.tile([C, 2, C], BF16, name="wl_sb")
        wc_sb = held.tile([C, 2, C], BF16, name="wc_sb")
        cur_sb = held.tile([C, N], BF16, name="cur_sb")
        near_sb = held.tile([C, N], BF16, name="near_sb")
        far_sb = held.tile([C, N], BF16, name="far_sb")
        bias_rows = held.tile([C, BLOCK], F32, name="bias_rows", align_bytes=64)
        bias_cols = held.tile([C, BLOCK], F32, name="bias_cols", align_bytes=64)
        bias = bias_cols[:, 0:1]
        offsets = held.tile([C, N // 16], U16, name="offsets")
        window = held.tile([C, S], F32, name="window")

        nc.gpsimd.memset(bias_rows[:], 0.0)

        nc.sync.dma_start(wl_sb[:], wl.rearrange("(h k) c -> k h c", h=2))
        nc.scalar.dma_start(bias_rows[::BLOCK, :], bl.rearrange("(q i) o -> q (i o)", i=BLOCK))
        nc.sync.dma_start(cur_sb[:, :HALF], cur[:, :HALF])
        nc.scalar.dma_start(near_sb[:, :HALF], near[:, :HALF])

        nc.sync.dma_start(wc_sb[:], wc.rearrange("(h k) c -> k h c", h=2))
        nc.scalar.dma_start(far_sb[:], far)

        nc.sync.dma_start(cur_sb[:, HALF:], cur[:, HALF:])
        nc.scalar.dma_start(near_sb[:, HALF:], near[:, HALF:])

        nc.sync.dma_start(offsets[:], offs)
        nc.sync.dma_start(window[:], base)

        tanh_in = held.tile([C, 1], F32, name="tanh_in")
        tanh_out = held.tile([C, 1], F32, name="tanh_out")
        nc.gpsimd.memset(tanh_in[:], 0.0)
        nc.scalar.activation(tanh_out[:], tanh_in[:], TANH)

        zeros = held.tile([C, WARM_COLS], BF16, name="zeros")
        nc.gpsimd.memset(zeros[:].bitcast(F32), 0.0)
        warm_ps = warm_psum.tile([C, WARM_COLS], F32, name="warm_ps")
        for i in range(WARM_MATMULS):
            nc.tensor.matmul(warm_ps[:], zeros[:, :C], zeros[:], start=True, stop=True)

        nc.vector.transpose(bias_cols[:], bias_rows[:])

        local = held.tile([C, N], F32, name="local")
        distant = held.tile([C, N], F32, name="distant")
        near_sum = held.tile([C, N], F32, name="near_sum")
        far_step = held.tile([C, N], F32, name="far_step")
        for first in range(0, N, HALF):
            chunks = [slice(j, j + CHUNK) for j in range(first, first + HALF, CHUNK)]

            for cols in chunks:
                local_ps = psum.tile([C, CHUNK], F32, name="local_ps")
                nc.tensor.matmul(local_ps[:], wl_sb[:, 0, :], cur_sb[:, cols], start=True, stop=False)
                nc.tensor.matmul(local_ps[:], wl_sb[:, 1, :], near_sb[:, cols], start=False, stop=True)
                nc.scalar.activation(local[:, cols], local_ps[:], TANH, bias=bias)
                nc.vector.scalar_tensor_tensor(
                    near_sum[:, cols], local[:, cols], GATE, cur_sb[:, cols], MULT, ADD
                )

            for cols in chunks:
                distant_ps = psum.tile([C, CHUNK], F32, name="distant_ps")
                nc.tensor.matmul(distant_ps[:], wc_sb[:, 0, :], cur_sb[:, cols], start=True, stop=False)
                nc.tensor.matmul(distant_ps[:], wc_sb[:, 1, :], far_sb[:, cols], start=False, stop=True)
                nc.scalar.activation(distant[:, cols], distant_ps[:], TANH)
                nc.vector.tensor_scalar(far_step[:, cols], distant[:, cols], GATE * DT, None, MULT)

        nc.sync.dma_start(out[:, :TOUCH], far_step[:, N - TOUCH :])
        nc.vector.tensor_tensor(window[:].indirect(offsets[:]), near_sum[:], far_step[:], ADD)
        nc.sync.dma_start(out, window[:])
